import numpy as np
import ml_dtypes


def mxq(x, axis, fmt="e4m3"):
    dtype, down = {"e4m3": (ml_dtypes.float8_e4m3fn, 7), "e5m2": (ml_dtypes.float8_e5m2, 14)}[fmt]
    v = np.moveaxis(np.asarray(x, np.float32).astype(ml_dtypes.bfloat16).astype(np.float64), axis, -1)
    blocks = v.reshape(v.shape[:-1] + (-1, 32))
    amax = np.abs(blocks).max(-1, keepdims=True)
    byte = np.maximum(np.where(amax > 0, np.frexp(amax)[1] - 1 + 127, 0) - down, 1)
    scale = np.exp2(byte - 127.0)
    codes = (blocks / scale).astype(np.float32).astype(dtype).astype(np.float64)
    return np.moveaxis((codes * scale).reshape(v.shape), -1, axis)


WIDE = False


def mx_kscale(k):
    if not WIDE:
        return np.ones(k)
    levels = np.array([10, -10, 5, -5, 0])
    a = np.random.permutation(np.resize(levels, k // 512 * 4)).reshape(k // 512, 4)
    idx = np.arange(k)
    return np.exp2(a[idx // 512, idx % 128 // 32])


BF16 = ml_dtypes.bfloat16


def bf(x):
    return np.asarray(x, np.float32).astype(BF16)


def f64(x):
    return np.asarray(x).astype(np.float64)


E2M1 = np.array([0.0, 0.5, 1.0, 1.5, 2.0, 3.0, 4.0, 6.0, -0.0, -0.5, -1.0, -1.5, -2.0, -3.0, -4.0, -6.0])


def pack_weight(w, fmt):
    k, n = w.shape
    w = f64(bf(w)).reshape(k // 32, 32, n)
    amax = np.abs(w).max(1)
    if fmt == "e4m3":
        byte = np.frexp(amax)[1] - 1 + 127 - 7
    else:
        mant, ex = np.frexp(amax / 6.0)
        byte = np.where(mant > 0.5, ex, ex - 1) + 127
    byte = np.clip(np.where(amax > 0, byte, 1), 1, 254)
    scaled = (w * np.exp2(127.0 - byte)[:, None, :]).reshape(k, n).astype(np.float32)
    by_word = np.ascontiguousarray(scaled.reshape(k // 512, 128, 4, n).transpose(0, 1, 3, 2))
    if fmt == "e4m3":
        words = by_word.astype(ml_dtypes.float8_e4m3fn).view(np.uint8)
    else:
        c = by_word.astype(ml_dtypes.float4_e2m1fn).view(np.uint8) & 0xF
        words = c[..., 0::2] | (c[..., 1::2] << 4)
    return np.ascontiguousarray(words), np.ascontiguousarray(byte.astype(np.uint8).reshape(k // 512, 16, n))


def unpack_weight(words, scales, fmt):
    g, p, n, _ = words.shape
    if fmt == "e4m3":
        vals = np.ascontiguousarray(words).view(ml_dtypes.float8_e4m3fn).astype(np.float64)
    else:
        nib = np.empty((g, p, n, 4), np.uint8)
        nib[..., 0::2] = words & 0xF
        nib[..., 1::2] = words >> 4
        vals = E2M1[nib]
    vals = vals * np.repeat(np.exp2(scales.astype(np.float64) - 127.0), 8, axis=1)[..., None]
    return vals.transpose(0, 1, 3, 2).reshape(g * 512, n)


B, N, D = 4, 512, 512
FMT = "e4m3"


def setup_inputs():
    s = mx_kscale(D)
    panel_embeddings = bf(np.random.standard_normal((B, N, D)) * s)
    words, scales = pack_weight(np.random.standard_normal((D, D)) * 4.0 / D / s[:, None] / s[None, :], FMT)
    b = bf(0.5 + 0.1 * np.random.standard_normal(1))
    return {"panel_embeddings": panel_embeddings,
            "W_words": words,
            "W_scales": scales,
            "b": b}


def reference(panel_embeddings, W_words, W_scales, b):
    xq = mxq(f64(panel_embeddings), 2, "e4m3")
    xw = xq @ unpack_weight(W_words, W_scales, FMT)
    scores = (mxq(xw, 2, "e4m3") @ xq.transpose(0, 2, 1)) + f64(b)
    n = panel_embeddings.shape[1]
    mask = ~np.eye(n, dtype=bool)
    return np.where(mask, scores, np.zeros_like(scores))

@@ -1,0 +1,156 @@
+from contextlib import ExitStack
+
+import concourse.mybir as mybir
+from concourse.masks import make_identity
+
+F32 = mybir.dt.float32
+BF16 = mybir.dt.bfloat16
+I32 = mybir.dt.int32
+U32 = mybir.dt.uint32
+U8 = mybir.dt.uint8
+FP8X4 = mybir.dt.float8_e4m3fn_x4
+
+P = 128
+PACK = 4
+BATCHES = 4
+PANELS = 512
+FEATURES = 512
+ROW_TILES = PANELS // P
+PARITIES = 2
+PSUM_BANKS = 8
+
+FLOPS = 2 * BATCHES * PANELS * FEATURES * FEATURES + 2 * BATCHES * PANELS * PANELS * FEATURES
+
+
+def tile_readingorderhead_kernel(tc, panel_embeddings, W_words, W_scales, b, out):
+    nc = tc.nc
+    with ExitStack() as ctx:
+        const = ctx.enter_context(tc.tile_pool(name="const", bufs=1))
+        per_batch = ctx.enter_context(tc.tile_pool(name="per_batch", bufs=BATCHES))
+        results = ctx.enter_context(tc.tile_pool(name="results", bufs=2 * ROW_TILES))
+        banks = ctx.enter_context(tc.psum_pool(name="banks", bufs=PSUM_BANKS))
+        ctx.enter_context(tc.manual_schedule())
+
+        def load_x(batch):
+            rows = per_batch.tile([P, ROW_TILES, FEATURES], BF16, name="x_rows")
+            nc.sync.dma_start(
+                out=rows[:], in_=panel_embeddings[batch].rearrange("(a p) k -> p a k", p=P)
+            )
+            return rows
+
+        x_rows = [load_x(0)]
+
+        w_codes = const.tile([P, PACK * FEATURES], U8, align_bytes=64)
+        nc.sync.dma_start(
+            out=w_codes[:].bitcast(I32),
+            in_=W_words[0].rearrange("p n t -> p (n t)").bitcast(I32),
+        )
+        w_scales = const.tile([P, FEATURES], U8, align_bytes=64)
+        nc.vector.memset(w_scales[:].bitcast(I32), 0)
+        for quadrant in range(4):
+            nc.sync.dma_start(
+                out=w_scales[32 * quadrant : 32 * quadrant + 4, :].bitcast(I32),
+                in_=W_scales[0, 4 * quadrant : 4 * quadrant + 4, :].bitcast(I32),
+            )
+
+        x_rows += [load_x(batch) for batch in range(1, BATCHES)]
+
+        bias_bf16 = const.tile([P, 1], BF16)
+        nc.scalar.dma_start(out=bias_bf16[:], in_=b.partition_broadcast(P))
+
+        identity = const.tile([P, P], F32)
+        make_identity(nc, identity[:])
+        off_diagonal = const.tile([P, (2 * ROW_TILES - 1) * P], F32)
+        nc.vector.memset(off_diagonal[:], 1.0)
+        nc.vector.tensor_scalar(
+            out=off_diagonal[:, (ROW_TILES - 1) * P : ROW_TILES * P],
+            in0=identity[:],
+            scalar1=-1.0,
+            scalar2=1.0,
+            op0=mybir.AluOpType.mult,
+            op1=mybir.AluOpType.add,
+        )
+        bias = const.tile([P, 1], F32)
+        nc.vector.tensor_copy(out=bias[:], in_=bias_bf16[:])
+
+        def quantise_along_rows(kind, words_of):
+            grouped = per_batch.tile([P, PACK * PANELS], BF16, name=kind + "_grouped", align_bytes=64)
+            grouped_words = grouped[:].bitcast(F32).rearrange(
+                "p (a i u) -> p a i u", a=ROW_TILES, u=PARITIES
+            )
+            for first in range(0, ROW_TILES, 2):
+                turned = banks.tile([P, 2, PARITIES, P], F32, name="bank")
+                for a in range(2):
+                    for u in range(PARITIES):
+                        nc.tensor.transpose(turned[:, a, u, :], words_of(first + a, u), identity[:])
+                nc.scalar.copy(
+                    out=grouped_words[:, first : first + 2],
+                    in_=turned[:].rearrange("p a u i -> p a i u"),
+                )
+            codes = per_batch.tile([P, PANELS], U32, name=kind + "_codes", align_bytes=64)
+            scales = per_batch.tile([P, PANELS], U8, name=kind + "_scales", align_bytes=64)
+            nc.vector.quantize_mx(out=codes[:].bitcast(FP8X4), scales=scales[:], in_=grouped[:])
+            return codes, scales
+
+        def mx_pass(stationary, moving, tile_index):
+            columns = slice(tile_index * P, (tile_index + 1) * P)
+            product = banks.tile([P, 512], F32, name="bank")
+            nc.tensor.matmul_mx(
+                out=product[:],
+                lhsT=stationary[0][:, columns].bitcast(FP8X4),
+                lhsT_scale=stationary[1][:, columns],
+                rhs=moving[0][:].bitcast(FP8X4),
+                rhs_scale=moving[1][:],
+                start=True,
+                stop=True,
+            )
+            return product
+
+        x_mx = {}
+        xw_rows = {}
+        xw_mx = {}
+
+        def quantise_x(batch):
+            words = x_rows[batch][:].bitcast(F32)
+            x_mx[batch] = quantise_along_rows(
+                "x", lambda a, u: words[:, a, u : FEATURES // 2 : PARITIES]
+            )
+
+        def x_times_w(batch):
+            rows = per_batch.tile([P, ROW_TILES, PARITIES, FEATURES // PARITIES], BF16, name="xw_rows")
+            for a in range(ROW_TILES):
+                product = mx_pass(x_mx[batch], (w_codes, w_scales), a)
+                nc.scalar.copy(
+                    out=rows[:, a].rearrange("i u (p e) -> i u p e", e=2),
+                    in_=product[:].rearrange("i (p u e) -> i u p e", u=PARITIES, e=2),
+                )
+            xw_rows[batch] = rows
+
+        def quantise_xw(batch):
+            words = xw_rows[batch][:].bitcast(F32)
+            xw_mx[batch] = quantise_along_rows("xw", lambda a, u: words[:, a, u, :])
+
+        def scores(batch):
+            for a in range(ROW_TILES):
+                product = mx_pass(xw_mx[batch], x_mx[batch], a)
+                first_column = (ROW_TILES - 1 - a) * P
+                masked = results.tile([P, PANELS], F32, name="masked")
+                nc.vector.scalar_tensor_tensor(
+                    out=masked[:],
+                    in0=product[:],
+                    scalar=bias[:, 0:1],
+                    in1=off_diagonal[:, first_column : first_column + PANELS],
+                    op0=mybir.AluOpType.add,
+                    op1=mybir.AluOpType.mult,
+                )
+                nc.sync.dma_start(out=out[batch, a * P : (a + 1) * P, :], in_=masked[:])
+
+        for step in range(BATCHES + 3):
+            if step < BATCHES:
+                quantise_x(step)
+            if 0 <= step - 2 < BATCHES:
+                quantise_xw(step - 2)
+            if 0 <= step - 1 < BATCHES:
+                x_times_w(step - 1)
+            if 0 <= step - 3 < BATCHES:
+                scores(step - 3)

@@ -17,6 +17,7 @@ PANELS = 512
 FEATURES = 512
 ROW_TILES = PANELS // P
 PARITIES = 2
+HALF = PANELS // 2
 PSUM_BANKS = 8
 
 FLOPS = 2 * BATCHES * PANELS * FEATURES * FEATURES + 2 * BATCHES * PANELS * PANELS * FEATURES
@@ -27,20 +28,20 @@ def tile_readingorderhead_kernel(tc, panel_embeddings, W_words, W_scales, b, out
     with ExitStack() as ctx:
         const = ctx.enter_context(tc.tile_pool(name="const", bufs=1))
         per_batch = ctx.enter_context(tc.tile_pool(name="per_batch", bufs=BATCHES))
-        results = ctx.enter_context(tc.tile_pool(name="results", bufs=2 * ROW_TILES))
+        results = ctx.enter_context(tc.tile_pool(name="results", bufs=4))
         banks = ctx.enter_context(tc.psum_pool(name="banks", bufs=PSUM_BANKS))
         ctx.enter_context(tc.manual_schedule())
 
         def load_x(batch):
             rows = per_batch.tile([P, ROW_TILES, FEATURES], BF16, name="x_rows")
-            nc.sync.dma_start(
-                out=rows[:], in_=panel_embeddings[batch].rearrange("(a p) k -> p a k", p=P)
-            )
+            panels = panel_embeddings[batch].rearrange("(a p) k -> p a k", p=P)
+            for first in range(0, ROW_TILES, 2):
+                nc.sync.dma_start(out=rows[:, first : first + 2], in_=panels[:, first : first + 2])
             return rows
 
         x_rows = [load_x(0)]
 
-        w_codes = const.tile([P, PACK * FEATURES], U8, align_bytes=64)
+        w_codes = const.tile([P, FEATURES], U32, align_bytes=64)
         nc.sync.dma_start(
             out=w_codes[:].bitcast(I32),
             in_=W_words[0].rearrange("p n t -> p (n t)").bitcast(I32),
@@ -60,18 +61,21 @@ def tile_readingorderhead_kernel(tc, panel_embeddings, W_words, W_scales, b, out
 
         identity = const.tile([P, P], F32)
         make_identity(nc, identity[:])
-        off_diagonal = const.tile([P, (2 * ROW_TILES - 1) * P], F32)
+        off_diagonal = const.tile([P, 2, HALF], F32)
         nc.vector.memset(off_diagonal[:], 1.0)
-        nc.vector.tensor_scalar(
-            out=off_diagonal[:, (ROW_TILES - 1) * P : ROW_TILES * P],
-            in0=identity[:],
-            scalar1=-1.0,
-            scalar2=1.0,
-            op0=mybir.AluOpType.mult,
-            op1=mybir.AluOpType.add,
-        )
+        for t in range(2):
+            nc.vector.tensor_scalar(
+                out=off_diagonal[:, t, t * P : (t + 1) * P],
+                in0=identity[:],
+                scalar1=-1.0,
+                scalar2=1.0,
+                op0=mybir.AluOpType.mult,
+                op1=mybir.AluOpType.add,
+            )
         bias = const.tile([P, 1], F32)
         nc.vector.tensor_copy(out=bias[:], in_=bias_bf16[:])
+
+        copy_of_half = (nc.scalar.copy, nc.vector.tensor_copy)
 
         def quantise_along_rows(kind, words_of):
             grouped = per_batch.tile([P, PACK * PANELS], BF16, name=kind + "_grouped", align_bytes=64)
@@ -83,7 +87,7 @@ def tile_readingorderhead_kernel(tc, panel_embeddings, W_words, W_scales, b, out
                 for a in range(2):
                     for u in range(PARITIES):
                         nc.tensor.transpose(turned[:, a, u, :], words_of(first + a, u), identity[:])
-                nc.scalar.copy(
+                copy_of_half[first // 2](
                     out=grouped_words[:, first : first + 2],
                     in_=turned[:].rearrange("p a u i -> p a i u"),
                 )
@@ -92,19 +96,17 @@ def tile_readingorderhead_kernel(tc, panel_embeddings, W_words, W_scales, b, out
             nc.vector.quantize_mx(out=codes[:].bitcast(FP8X4), scales=scales[:], in_=grouped[:])
             return codes, scales
 
-        def mx_pass(stationary, moving, tile_index):
+        def mx_pass(product, stationary, tile_index, moving, moving_columns):
             columns = slice(tile_index * P, (tile_index + 1) * P)
-            product = banks.tile([P, 512], F32, name="bank")
             nc.tensor.matmul_mx(
-                out=product[:],
+                out=product,
                 lhsT=stationary[0][:, columns].bitcast(FP8X4),
                 lhsT_scale=stationary[1][:, columns],
-                rhs=moving[0][:].bitcast(FP8X4),
-                rhs_scale=moving[1][:],
+                rhs=moving[0][:, moving_columns].bitcast(FP8X4),
+                rhs_scale=moving[1][:, moving_columns],
                 start=True,
                 stop=True,
             )
-            return product
 
         x_mx = {}
         xw_rows = {}
@@ -119,8 +121,10 @@ def tile_readingorderhead_kernel(tc, panel_embeddings, W_words, W_scales, b, out
         def x_times_w(batch):
             rows = per_batch.tile([P, ROW_TILES, PARITIES, FEATURES // PARITIES], BF16, name="xw_rows")
             for a in range(ROW_TILES):
-                product = mx_pass(x_mx[batch], (w_codes, w_scales), a)
-                nc.scalar.copy(
+                product = banks.tile([P, FEATURES], F32, name="bank")
+                mx_pass(product[:], x_mx[batch], a, (w_codes, w_scales), slice(0, FEATURES))
+                copy = nc.scalar.copy if a < ROW_TILES - 1 else nc.vector.tensor_copy
+                copy(
                     out=rows[:, a].rearrange("i u (p e) -> i u p e", e=2),
                     in_=product[:].rearrange("i (p u e) -> i u p e", u=PARITIES, e=2),
                 )
@@ -131,19 +135,33 @@ def tile_readingorderhead_kernel(tc, panel_embeddings, W_words, W_scales, b, out
             xw_mx[batch] = quantise_along_rows("xw", lambda a, u: words[:, a, u, :])
 
         def scores(batch):
-            for a in range(ROW_TILES):
-                product = mx_pass(xw_mx[batch], x_mx[batch], a)
-                first_column = (ROW_TILES - 1 - a) * P
-                masked = results.tile([P, PANELS], F32, name="masked")
+            for pair in range(ROW_TILES // 2):
+                near = slice(pair * HALF, (pair + 1) * HALF)
+                far = slice((1 - pair) * HALF, (2 - pair) * HALF)
+                finished = results.tile([P, 2, PANELS], F32, name="finished")
+                with_diagonal = banks.tile([P, 2, HALF], F32, name="bank")
+                for t in range(2):
+                    mx_pass(with_diagonal[:, t, :], xw_mx[batch], 2 * pair + t, x_mx[batch], near)
                 nc.vector.scalar_tensor_tensor(
-                    out=masked[:],
-                    in0=product[:],
+                    out=finished[:, :, near],
+                    in0=with_diagonal[:],
                     scalar=bias[:, 0:1],
-                    in1=off_diagonal[:, first_column : first_column + PANELS],
+                    in1=off_diagonal[:],
                     op0=mybir.AluOpType.add,
                     op1=mybir.AluOpType.mult,
                 )
-                nc.sync.dma_start(out=out[batch, a * P : (a + 1) * P, :], in_=masked[:])
+                without_diagonal = banks.tile([P, 2, HALF], F32, name="bank")
+                for t in range(2):
+                    mx_pass(without_diagonal[:, t, :], xw_mx[batch], 2 * pair + t, x_mx[batch], far)
+                nc.scalar.activation(
+                    out=finished[:, :, far],
+                    in_=without_diagonal[:],
+                    func=mybir.ActivationFunctionType.Identity,
+                    bias=bias[:, 0:1],
+                )
+                nc.sync.dma_start(
+                    out=out[batch, near, :].rearrange("(t p) j -> p t j", p=P), in_=finished[:]
+                )
 
         for step in range(BATCHES + 3):
             if step < BATCHES:

@@ -82,6 +82,8 @@ def tile_readingorderhead_kernel(tc, panel_embeddings, W_words, W_scales, b, out
             grouped_words = grouped[:].bitcast(F32).rearrange(
                 "p (a i u) -> p a i u", a=ROW_TILES, u=PARITIES
             )
+            codes = per_batch.tile([P, PANELS], U32, name=kind + "_codes", align_bytes=64)
+            scales = per_batch.tile([P, PANELS], U8, name=kind + "_scales", align_bytes=64)
             for first in range(0, ROW_TILES, 2):
                 turned = banks.tile([P, 2, PARITIES, P], F32, name="bank")
                 for a in range(2):
@@ -91,9 +93,13 @@ def tile_readingorderhead_kernel(tc, panel_embeddings, W_words, W_scales, b, out
                     out=grouped_words[:, first : first + 2],
                     in_=turned[:].rearrange("p a u i -> p a i u"),
                 )
-            codes = per_batch.tile([P, PANELS], U32, name=kind + "_codes", align_bytes=64)
-            scales = per_batch.tile([P, PANELS], U8, name=kind + "_scales", align_bytes=64)
-            nc.vector.quantize_mx(out=codes[:].bitcast(FP8X4), scales=scales[:], in_=grouped[:])
+            for first in range(0, ROW_TILES, 2):
+                panels = slice(first * P, (first + 2) * P)
+                nc.vector.quantize_mx(
+                    out=codes[:, panels].bitcast(FP8X4),
+                    scales=scales[:, panels],
+                    in_=grouped[:, PACK * first * P : PACK * (first + 2) * P],
+                )
             return codes, scales
 
         def mx_pass(product, stationary, tile_index, moving, moving_columns):

@@ -75,7 +75,11 @@ def tile_readingorderhead_kernel(tc, panel_embeddings, W_words, W_scales, b, out
         bias = const.tile([P, 1], F32)
         nc.vector.tensor_copy(out=bias[:], in_=bias_bf16[:])
 
-        copy_of_half = (nc.scalar.copy, nc.vector.tensor_copy)
+        copies_of = {
+            "x": (nc.scalar.copy, nc.vector.tensor_copy),
+            "xw": (nc.scalar.copy, nc.scalar.copy),
+            "x @ W": (nc.vector.tensor_copy, nc.scalar.copy),
+        }
 
         def quantise_along_rows(kind, words_of):
             grouped = per_batch.tile([P, PACK * PANELS], BF16, name=kind + "_grouped", align_bytes=64)
@@ -89,7 +93,7 @@ def tile_readingorderhead_kernel(tc, panel_embeddings, W_words, W_scales, b, out
                 for a in range(2):
                     for u in range(PARITIES):
                         nc.tensor.transpose(turned[:, a, u, :], words_of(first + a, u), identity[:])
-                copy_of_half[first // 2](
+                copies_of[kind][first // 2](
                     out=grouped_words[:, first : first + 2],
                     in_=turned[:].rearrange("p a u i -> p a i u"),
                 )
@@ -129,8 +133,7 @@ def tile_readingorderhead_kernel(tc, panel_embeddings, W_words, W_scales, b, out
             for a in range(ROW_TILES):
                 product = banks.tile([P, FEATURES], F32, name="bank")
                 mx_pass(product[:], x_mx[batch], a, (w_codes, w_scales), slice(0, FEATURES))
-                copy = nc.scalar.copy if a < ROW_TILES - 1 else nc.vector.tensor_copy
-                copy(
+                copies_of["x @ W"][a % 2](
                     out=rows[:, a].rearrange("i u (p e) -> i u p e", e=2),
                     in_=product[:].rearrange("i (p u e) -> i u p e", u=PARITIES, e=2),
                 )
@@ -169,12 +172,12 @@ def tile_readingorderhead_kernel(tc, panel_embeddings, W_words, W_scales, b, out
                     out=out[batch, near, :].rearrange("(t p) j -> p t j", p=P), in_=finished[:]
                 )
 
-        for step in range(BATCHES + 3):
+        for step in range(BATCHES + 2):
             if step < BATCHES:
                 quantise_x(step)
             if 0 <= step - 2 < BATCHES:
                 quantise_xw(step - 2)
             if 0 <= step - 1 < BATCHES:
                 x_times_w(step - 1)
-            if 0 <= step - 3 < BATCHES:
-                scores(step - 3)
+            if 0 <= step - 2 < BATCHES:
+                scores(step - 2)

@@ -57,7 +57,8 @@ def tile_readingorderhead_kernel(tc, panel_embeddings, W_words, W_scales, b, out
         x_rows += [load_x(batch) for batch in range(1, BATCHES)]
 
         bias_bf16 = const.tile([P, 1], BF16)
-        nc.scalar.dma_start(out=bias_bf16[:], in_=b.partition_broadcast(P))
+        nc.sync.dma_start(out=bias_bf16[:], in_=b.partition_broadcast(P))
+        bias = const.tile([P, 1], F32)
 
         identity = const.tile([P, P], F32)
         make_identity(nc, identity[:])
@@ -72,14 +73,9 @@ def tile_readingorderhead_kernel(tc, panel_embeddings, W_words, W_scales, b, out
                 op0=mybir.AluOpType.mult,
                 op1=mybir.AluOpType.add,
             )
-        bias = const.tile([P, 1], F32)
-        nc.vector.tensor_copy(out=bias[:], in_=bias_bf16[:])
+        nc.gpsimd.tensor_copy(out=bias[:], in_=bias_bf16[:])
 
-        copies_of = {
-            "x": (nc.scalar.copy, nc.vector.tensor_copy),
-            "xw": (nc.scalar.copy, nc.scalar.copy),
-            "x @ W": (nc.vector.tensor_copy, nc.scalar.copy),
-        }
+        copy_of_half = (nc.scalar.copy, nc.vector.tensor_copy)
 
         def quantise_along_rows(kind, words_of):
             grouped = per_batch.tile([P, PACK * PANELS], BF16, name=kind + "_grouped", align_bytes=64)
@@ -93,7 +89,7 @@ def tile_readingorderhead_kernel(tc, panel_embeddings, W_words, W_scales, b, out
                 for a in range(2):
                     for u in range(PARITIES):
                         nc.tensor.transpose(turned[:, a, u, :], words_of(first + a, u), identity[:])
-                copies_of[kind][first // 2](
+                copy_of_half[first // 2](
                     out=grouped_words[:, first : first + 2],
                     in_=turned[:].rearrange("p a u i -> p a i u"),
                 )
@@ -133,7 +129,8 @@ def tile_readingorderhead_kernel(tc, panel_embeddings, W_words, W_scales, b, out
             for a in range(ROW_TILES):
                 product = banks.tile([P, FEATURES], F32, name="bank")
                 mx_pass(product[:], x_mx[batch], a, (w_codes, w_scales), slice(0, FEATURES))
-                copies_of["x @ W"][a % 2](
+                copy = nc.scalar.copy if a < ROW_TILES - 1 else nc.vector.tensor_copy
+                copy(
                     out=rows[:, a].rearrange("i u (p e) -> i u p e", e=2),
                     in_=product[:].rearrange("i (p u e) -> i u p e", u=PARITIES, e=2),
                 )
@@ -172,12 +169,12 @@ def tile_readingorderhead_kernel(tc, panel_embeddings, W_words, W_scales, b, out
                     out=out[batch, near, :].rearrange("(t p) j -> p t j", p=P), in_=finished[:]
                 )
 
-        for step in range(BATCHES + 2):
+        for step in range(BATCHES + 3):
             if step < BATCHES:
                 quantise_x(step)
             if 0 <= step - 2 < BATCHES:
                 quantise_xw(step - 2)
             if 0 <= step - 1 < BATCHES:
                 x_times_w(step - 1)
-            if 0 <= step - 2 < BATCHES:
-                scores(step - 2)
+            if 0 <= step - 3 < BATCHES:
+                scores(step - 3)

@@ -18,6 +18,7 @@ FEATURES = 512
 ROW_TILES = PANELS // P
 PARITIES = 2
 HALF = PANELS // 2
+PAIRS = ROW_TILES // 2
 PSUM_BANKS = 8
 
 FLOPS = 2 * BATCHES * PANELS * FEATURES * FEATURES + 2 * BATCHES * PANELS * PANELS * FEATURES
@@ -28,33 +29,39 @@ def tile_readingorderhead_kernel(tc, panel_embeddings, W_words, W_scales, b, out
     with ExitStack() as ctx:
         const = ctx.enter_context(tc.tile_pool(name="const", bufs=1))
         per_batch = ctx.enter_context(tc.tile_pool(name="per_batch", bufs=BATCHES))
-        results = ctx.enter_context(tc.tile_pool(name="results", bufs=4))
+        results = ctx.enter_context(tc.tile_pool(name="results", bufs=BATCHES * PAIRS))
         banks = ctx.enter_context(tc.psum_pool(name="banks", bufs=PSUM_BANKS))
         ctx.enter_context(tc.manual_schedule())
 
-        def load_x(batch):
-            rows = per_batch.tile([P, ROW_TILES, FEATURES], BF16, name="x_rows")
+        x_rows = []
+
+        def load_x(batch, pair):
+            if pair == 0:
+                rows = per_batch.tile([P, ROW_TILES, FEATURES], BF16, name="x_rows")
+                x_rows.append(rows)
             panels = panel_embeddings[batch].rearrange("(a p) k -> p a k", p=P)
-            for first in range(0, ROW_TILES, 2):
-                nc.sync.dma_start(out=rows[:, first : first + 2], in_=panels[:, first : first + 2])
-            return rows
-
-        x_rows = [load_x(0)]
-
-        w_codes = const.tile([P, FEATURES], U32, align_bytes=64)
-        nc.sync.dma_start(
-            out=w_codes[:].bitcast(I32),
-            in_=W_words[0].rearrange("p n t -> p (n t)").bitcast(I32),
-        )
-        w_scales = const.tile([P, FEATURES], U8, align_bytes=64)
-        nc.vector.memset(w_scales[:].bitcast(I32), 0)
-        for quadrant in range(4):
             nc.sync.dma_start(
-                out=w_scales[32 * quadrant : 32 * quadrant + 4, :].bitcast(I32),
-                in_=W_scales[0, 4 * quadrant : 4 * quadrant + 4, :].bitcast(I32),
+                out=x_rows[batch][:, 2 * pair : 2 * pair + 2], in_=panels[:, 2 * pair : 2 * pair + 2]
             )
 
-        x_rows += [load_x(batch) for batch in range(1, BATCHES)]
+        load_x(0, 0)
+
+        w_scales_as_sent = const.tile([P, FEATURES], U8, align_bytes=64)
+        nc.vector.memset(w_scales_as_sent[:].bitcast(I32), 0)
+        for quadrant in range(4):
+            nc.sync.dma_start(
+                out=w_scales_as_sent[32 * quadrant : 32 * quadrant + 4, :].bitcast(I32),
+                in_=W_scales[0, 4 * quadrant : 4 * quadrant + 4, :].bitcast(I32),
+            )
+        w_codes_as_sent = const.tile([P, FEATURES], U32, align_bytes=64)
+        nc.sync.dma_start(
+            out=w_codes_as_sent[:].bitcast(I32),
+            in_=W_words[0].rearrange("p n t -> p (n t)").bitcast(I32),
+        )
+        load_x(0, 1)
+        for batch in range(1, BATCHES):
+            for pair in range(PAIRS):
+                load_x(batch, pair)
 
         bias_bf16 = const.tile([P, 1], BF16)
         nc.sync.dma_start(out=bias_bf16[:], in_=b.partition_broadcast(P))
@@ -75,32 +82,16 @@ def tile_readingorderhead_kernel(tc, panel_embeddings, W_words, W_scales, b, out
             )
         nc.gpsimd.tensor_copy(out=bias[:], in_=bias_bf16[:])
 
-        copy_of_half = (nc.scalar.copy, nc.vector.tensor_copy)
-
-        def quantise_along_rows(kind, words_of):
-            grouped = per_batch.tile([P, PACK * PANELS], BF16, name=kind + "_grouped", align_bytes=64)
-            grouped_words = grouped[:].bitcast(F32).rearrange(
-                "p (a i u) -> p a i u", a=ROW_TILES, u=PARITIES
-            )
-            codes = per_batch.tile([P, PANELS], U32, name=kind + "_codes", align_bytes=64)
-            scales = per_batch.tile([P, PANELS], U8, name=kind + "_scales", align_bytes=64)
-            for first in range(0, ROW_TILES, 2):
-                turned = banks.tile([P, 2, PARITIES, P], F32, name="bank")
-                for a in range(2):
-                    for u in range(PARITIES):
-                        nc.tensor.transpose(turned[:, a, u, :], words_of(first + a, u), identity[:])
-                copy_of_half[first // 2](
-                    out=grouped_words[:, first : first + 2],
-                    in_=turned[:].rearrange("p a u i -> p a i u"),
-                )
-            for first in range(0, ROW_TILES, 2):
-                panels = slice(first * P, (first + 2) * P)
-                nc.vector.quantize_mx(
-                    out=codes[:, panels].bitcast(FP8X4),
-                    scales=scales[:, panels],
-                    in_=grouped[:, PACK * first * P : PACK * (first + 2) * P],
-                )
-            return codes, scales
+        w_scales = const.tile([P, FEATURES], U8, align_bytes=64)
+        nc.vector.tensor_copy(
+            out=w_scales[:].rearrange("p (t m) -> p t m", t=PACK),
+            in_=w_scales_as_sent[:].rearrange("p (m t) -> p t m", t=PACK),
+        )
+        w_codes = const.tile([P, FEATURES], U32, align_bytes=64)
+        nc.vector.tensor_copy(
+            out=w_codes[:].bitcast(I32).rearrange("p (t m) -> p t m", t=PACK),
+            in_=w_codes_as_sent[:].bitcast(I32).rearrange("p (m t) -> p t m", t=PACK),
+        )
 
         def mx_pass(product, stationary, tile_index, moving, moving_columns):
             columns = slice(tile_index * P, (tile_index + 1) * P)
@@ -114,67 +105,96 @@ def tile_readingorderhead_kernel(tc, panel_embeddings, W_words, W_scales, b, out
                 stop=True,
             )
 
-        x_mx = {}
-        xw_rows = {}
-        xw_mx = {}
+        def new_operand(kind):
+            grouped = per_batch.tile([P, PACK * PANELS], BF16, name=kind + "_grouped", align_bytes=64)
+            codes = per_batch.tile([P, PANELS], U32, name=kind + "_codes", align_bytes=64)
+            scales = per_batch.tile([P, PANELS], U8, name=kind + "_scales", align_bytes=64)
+            return grouped, codes, scales
 
-        def quantise_x(batch):
-            words = x_rows[batch][:].bitcast(F32)
-            x_mx[batch] = quantise_along_rows(
-                "x", lambda a, u: words[:, a, u : FEATURES // 2 : PARITIES]
+        def quantise(operand, pair):
+            grouped, codes, scales = operand
+            panels = slice(pair * HALF, (pair + 1) * HALF)
+            nc.vector.quantize_mx(
+                out=codes[:, panels].bitcast(FP8X4),
+                scales=scales[:, panels],
+                in_=grouped[:, PACK * pair * HALF : PACK * (pair + 1) * HALF],
             )
 
-        def x_times_w(batch):
-            rows = per_batch.tile([P, ROW_TILES, PARITIES, FEATURES // PARITIES], BF16, name="xw_rows")
+        x_mx = {}
+        xw_mx = {}
+
+        def turn_x(batch):
+            x_mx[batch] = new_operand("x")
+            grouped_words = x_mx[batch][0][:].bitcast(F32).rearrange(
+                "p (a i u) -> p a i u", a=ROW_TILES, u=PARITIES
+            )
+            words = x_rows[batch][:].bitcast(F32)
+            for pair in range(PAIRS):
+                turned = banks.tile([P, 2, PARITIES, P], F32, name="bank")
+                for a in range(2):
+                    for u in range(PARITIES):
+                        nc.tensor.transpose(
+                            turned[:, a, u, :],
+                            words[:, 2 * pair + a, u : FEATURES // 2 : PARITIES],
+                            identity[:],
+                        )
+                nc.scalar.copy(
+                    out=grouped_words[:, 2 * pair : 2 * pair + 2],
+                    in_=turned[:].rearrange("p a u i -> p a i u"),
+                )
+
+        def w_times_x(batch):
+            xw_mx[batch] = new_operand("xw")
+            grouped = xw_mx[batch][0]
             for a in range(ROW_TILES):
-                product = banks.tile([P, FEATURES], F32, name="bank")
-                mx_pass(product[:], x_mx[batch], a, (w_codes, w_scales), slice(0, FEATURES))
-                copy = nc.scalar.copy if a < ROW_TILES - 1 else nc.vector.tensor_copy
+                product = banks.tile([P, PACK, P], F32, name="bank")
+                for t in range(PACK):
+                    mx_pass(
+                        product[:, t, :], (w_codes, w_scales), t, x_mx[batch][1:], slice(a * P, (a + 1) * P)
+                    )
+                copy = nc.scalar.copy if a < 2 else nc.vector.tensor_copy
                 copy(
-                    out=rows[:, a].rearrange("i u (p e) -> i u p e", e=2),
-                    in_=product[:].rearrange("i (p u e) -> i u p e", u=PARITIES, e=2),
-                )
-            xw_rows[batch] = rows
-
-        def quantise_xw(batch):
-            words = xw_rows[batch][:].bitcast(F32)
-            xw_mx[batch] = quantise_along_rows("xw", lambda a, u: words[:, a, u, :])
-
-        def scores(batch):
-            for pair in range(ROW_TILES // 2):
-                near = slice(pair * HALF, (pair + 1) * HALF)
-                far = slice((1 - pair) * HALF, (2 - pair) * HALF)
-                finished = results.tile([P, 2, PANELS], F32, name="finished")
-                with_diagonal = banks.tile([P, 2, HALF], F32, name="bank")
-                for t in range(2):
-                    mx_pass(with_diagonal[:, t, :], xw_mx[batch], 2 * pair + t, x_mx[batch], near)
-                nc.vector.scalar_tensor_tensor(
-                    out=finished[:, :, near],
-                    in0=with_diagonal[:],
-                    scalar=bias[:, 0:1],
-                    in1=off_diagonal[:],
-                    op0=mybir.AluOpType.add,
-                    op1=mybir.AluOpType.mult,
-                )
-                without_diagonal = banks.tile([P, 2, HALF], F32, name="bank")
-                for t in range(2):
-                    mx_pass(without_diagonal[:, t, :], xw_mx[batch], 2 * pair + t, x_mx[batch], far)
-                nc.scalar.activation(
-                    out=finished[:, :, far],
-                    in_=without_diagonal[:],
-                    func=mybir.ActivationFunctionType.Identity,
-                    bias=bias[:, 0:1],
-                )
-                nc.sync.dma_start(
-                    out=out[batch, near, :].rearrange("(t p) j -> p t j", p=P), in_=finished[:]
+                    out=grouped[:, PACK * a * P : PACK * (a + 1) * P].rearrange("p (i t) -> p i t", t=PACK),
+                    in_=product[:].rearrange("p t i -> p i t"),
                 )
 
-        for step in range(BATCHES + 3):
+        def scores(batch, pair):
+            near = slice(pair * HALF, (pair + 1) * HALF)
+            far = slice((1 - pair) * HALF, (2 - pair) * HALF)
+            finished = results.tile([P, 2, PANELS], F32, name="finished")
+            with_diagonal = banks.tile([P, 2, HALF], F32, name="bank")
+            for t in range(2):
+                mx_pass(with_diagonal[:, t, :], xw_mx[batch][1:], 2 * pair + t, x_mx[batch][1:], near)
+            nc.vector.scalar_tensor_tensor(
+                out=finished[:, :, near],
+                in0=with_diagonal[:],
+                scalar=bias[:, 0:1],
+                in1=off_diagonal[:],
+                op0=mybir.AluOpType.add,
+                op1=mybir.AluOpType.mult,
+            )
+            without_diagonal = banks.tile([P, 2, HALF], F32, name="bank")
+            for t in range(2):
+                mx_pass(without_diagonal[:, t, :], xw_mx[batch][1:], 2 * pair + t, x_mx[batch][1:], far)
+            nc.scalar.activation(
+                out=finished[:, :, far],
+                in_=without_diagonal[:],
+                func=mybir.ActivationFunctionType.Identity,
+                bias=bias[:, 0:1],
+            )
+            nc.sync.dma_start(
+                out=out[batch, near, :].rearrange("(t p) j -> p t j", p=P), in_=finished[:]
+            )
+
+        for step in range(BATCHES + 2):
             if step < BATCHES:
-                quantise_x(step)
-            if 0 <= step - 2 < BATCHES:
-                quantise_xw(step - 2)
+                turn_x(step)
+                for pair in range(PAIRS):
+                    quantise(x_mx[step], pair)
             if 0 <= step - 1 < BATCHES:
-                x_times_w(step - 1)
-            if 0 <= step - 3 < BATCHES:
-                scores(step - 3)
+                w_times_x(step - 1)
+            for pair in range(PAIRS):
+                if 0 <= step - 1 < BATCHES:
+                    quantise(xw_mx[step - 1], pair)
+                if 0 <= step - 2 < BATCHES:
+                    scores(step - 2, pair)

@@ -143,16 +143,18 @@ def tile_readingorderhead_kernel(tc, panel_embeddings, W_words, W_scales, b, out
                     in_=turned[:].rearrange("p a u i -> p a i u"),
                 )
 
-        def w_times_x(batch):
-            xw_mx[batch] = new_operand("xw")
+        def w_times_x(batch, pair):
+            if pair == 0:
+                xw_mx[batch] = new_operand("xw")
             grouped = xw_mx[batch][0]
-            for a in range(ROW_TILES):
+            for a in range(2 * pair, 2 * pair + 2):
                 product = banks.tile([P, PACK, P], F32, name="bank")
                 for t in range(PACK):
                     mx_pass(
                         product[:, t, :], (w_codes, w_scales), t, x_mx[batch][1:], slice(a * P, (a + 1) * P)
                     )
-                copy = nc.scalar.copy if a < 2 else nc.vector.tensor_copy
+                to_vector = a == ROW_TILES - 1 if batch == BATCHES - 1 else a % 2 == 1
+                copy = nc.vector.tensor_copy if to_vector else nc.scalar.copy
                 copy(
                     out=grouped[:, PACK * a * P : PACK * (a + 1) * P].rearrange("p (i t) -> p i t", t=PACK),
                     in_=product[:].rearrange("p t i -> p i t"),
@@ -161,40 +163,41 @@ def tile_readingorderhead_kernel(tc, panel_embeddings, W_words, W_scales, b, out
         def scores(batch, pair):
             near = slice(pair * HALF, (pair + 1) * HALF)
             far = slice((1 - pair) * HALF, (2 - pair) * HALF)
-            finished = results.tile([P, 2, PANELS], F32, name="finished")
+            rows = out[batch, near, :].rearrange("(t p) j -> p t j", p=P)
             with_diagonal = banks.tile([P, 2, HALF], F32, name="bank")
             for t in range(2):
                 mx_pass(with_diagonal[:, t, :], xw_mx[batch][1:], 2 * pair + t, x_mx[batch][1:], near)
+            masked = results.tile([P, 2, HALF], F32, name="masked")
             nc.vector.scalar_tensor_tensor(
-                out=finished[:, :, near],
+                out=masked[:],
                 in0=with_diagonal[:],
                 scalar=bias[:, 0:1],
                 in1=off_diagonal[:],
                 op0=mybir.AluOpType.add,
                 op1=mybir.AluOpType.mult,
             )
+            nc.sync.dma_start(out=rows[:, :, near], in_=masked[:])
             without_diagonal = banks.tile([P, 2, HALF], F32, name="bank")
             for t in range(2):
                 mx_pass(without_diagonal[:, t, :], xw_mx[batch][1:], 2 * pair + t, x_mx[batch][1:], far)
+            unmasked = results.tile([P, 2, HALF], F32, name="unmasked")
             nc.scalar.activation(
-                out=finished[:, :, far],
+                out=unmasked[:],
                 in_=without_diagonal[:],
                 func=mybir.ActivationFunctionType.Identity,
                 bias=bias[:, 0:1],
             )
-            nc.sync.dma_start(
-                out=out[batch, near, :].rearrange("(t p) j -> p t j", p=P), in_=finished[:]
-            )
+            nc.sync.dma_start(out=rows[:, :, far], in_=unmasked[:])
 
         for step in range(BATCHES + 2):
             if step < BATCHES:
                 turn_x(step)
                 for pair in range(PAIRS):
                     quantise(x_mx[step], pair)
-            if 0 <= step - 1 < BATCHES:
-                w_times_x(step - 1)
             for pair in range(PAIRS):
                 if 0 <= step - 1 < BATCHES:
-                    quantise(xw_mx[step - 1], pair)
+                    w_times_x(step - 1, pair)
                 if 0 <= step - 2 < BATCHES:
                     scores(step - 2, pair)
+                if 0 <= step - 1 < BATCHES:
+                    quantise(xw_mx[step - 1], pair)

@@ -39,13 +39,12 @@ def tile_readingorderhead_kernel(tc, panel_embeddings, W_words, W_scales, b, out
             if pair == 0:
                 rows = per_batch.tile([P, ROW_TILES, FEATURES], BF16, name="x_rows")
                 x_rows.append(rows)
-            panels = panel_embeddings[batch].rearrange("(a p) k -> p a k", p=P)
-            nc.sync.dma_start(
-                out=x_rows[batch][:, 2 * pair : 2 * pair + 2], in_=panels[:, 2 * pair : 2 * pair + 2]
-            )
+            panels = panel_embeddings[batch].rearrange("(h p t) k -> p h t k", h=PAIRS, t=2)
+            nc.sync.dma_start(out=x_rows[batch][:, 2 * pair : 2 * pair + 2], in_=panels[:, pair])
 
         load_x(0, 0)
-
+        load_x(0, 1)
+        load_x(1, 0)
         w_scales_as_sent = const.tile([P, FEATURES], U8, align_bytes=64)
         nc.vector.memset(w_scales_as_sent[:].bitcast(I32), 0)
         for quadrant in range(4):
@@ -58,10 +57,11 @@ def tile_readingorderhead_kernel(tc, panel_embeddings, W_words, W_scales, b, out
             out=w_codes_as_sent[:].bitcast(I32),
             in_=W_words[0].rearrange("p n t -> p (n t)").bitcast(I32),
         )
-        load_x(0, 1)
-        for batch in range(1, BATCHES):
-            for pair in range(PAIRS):
-                load_x(batch, pair)
+        load_x(1, 1)
+        load_x(2, 0)
+        load_x(2, 1)
+        load_x(3, 0)
+        load_x(3, 1)
 
         bias_bf16 = const.tile([P, 1], BF16)
         nc.sync.dma_start(out=bias_bf16[:], in_=b.partition_broadcast(P))
@@ -126,7 +126,7 @@ def tile_readingorderhead_kernel(tc, panel_embeddings, W_words, W_scales, b, out
         def turn_x(batch):
             x_mx[batch] = new_operand("x")
             grouped_words = x_mx[batch][0][:].bitcast(F32).rearrange(
-                "p (a i u) -> p a i u", a=ROW_TILES, u=PARITIES
+                "p (h i w) -> p h i w", h=PAIRS, w=2 * PARITIES
             )
             words = x_rows[batch][:].bitcast(F32)
             for pair in range(PAIRS):
@@ -139,8 +139,8 @@ def tile_readingorderhead_kernel(tc, panel_embeddings, W_words, W_scales, b, out
                             identity[:],
                         )
                 nc.scalar.copy(
-                    out=grouped_words[:, 2 * pair : 2 * pair + 2],
-                    in_=turned[:].rearrange("p a u i -> p a i u"),
+                    out=grouped_words[:, pair],
+                    in_=turned[:].rearrange("p t u i -> p i (t u)"),
                 )
 
         def w_times_x(batch, pair):

@@ -73,7 +73,7 @@ def tile_readingorderhead_kernel(tc, panel_embeddings, W_words, W_scales, b, out
         nc.vector.memset(off_diagonal[:], 1.0)
         for t in range(2):
             nc.vector.tensor_scalar(
-                out=off_diagonal[:, t, t * P : (t + 1) * P],
+                out=off_diagonal[:, t, t:HALF:2],
                 in0=identity[:],
                 scalar1=-1.0,
                 scalar2=1.0,
@@ -146,7 +146,9 @@ def tile_readingorderhead_kernel(tc, panel_embeddings, W_words, W_scales, b, out
         def w_times_x(batch, pair):
             if pair == 0:
                 xw_mx[batch] = new_operand("xw")
-            grouped = xw_mx[batch][0]
+            places = xw_mx[batch][0][:].rearrange(
+                "p (h e c i t) -> p h e c i t", h=PAIRS, e=2, c=2, t=PACK
+            )
             for a in range(2 * pair, 2 * pair + 2):
                 product = banks.tile([P, PACK, P], F32, name="bank")
                 for t in range(PACK):
@@ -156,38 +158,38 @@ def tile_readingorderhead_kernel(tc, panel_embeddings, W_words, W_scales, b, out
                 to_vector = a == ROW_TILES - 1 if batch == BATCHES - 1 else a % 2 == 1
                 copy = nc.vector.tensor_copy if to_vector else nc.scalar.copy
                 copy(
-                    out=grouped[:, PACK * a * P : PACK * (a + 1) * P].rearrange("p (i t) -> p i t", t=PACK),
-                    in_=product[:].rearrange("p t i -> p i t"),
+                    out=places[:, pair, :, a % 2],
+                    in_=product[:].rearrange("p t (i e) -> p e i t", e=2),
                 )
 
         def scores(batch, pair):
             near = slice(pair * HALF, (pair + 1) * HALF)
             far = slice((1 - pair) * HALF, (2 - pair) * HALF)
-            rows = out[batch, near, :].rearrange("(t p) j -> p t j", p=P)
+            finished = results.tile([P, 2, PANELS], F32, name="finished")
             with_diagonal = banks.tile([P, 2, HALF], F32, name="bank")
             for t in range(2):
                 mx_pass(with_diagonal[:, t, :], xw_mx[batch][1:], 2 * pair + t, x_mx[batch][1:], near)
-            masked = results.tile([P, 2, HALF], F32, name="masked")
             nc.vector.scalar_tensor_tensor(
-                out=masked[:],
+                out=finished[:, :, near],
                 in0=with_diagonal[:],
                 scalar=bias[:, 0:1],
                 in1=off_diagonal[:],
                 op0=mybir.AluOpType.add,
                 op1=mybir.AluOpType.mult,
             )
-            nc.sync.dma_start(out=rows[:, :, near], in_=masked[:])
             without_diagonal = banks.tile([P, 2, HALF], F32, name="bank")
             for t in range(2):
                 mx_pass(without_diagonal[:, t, :], xw_mx[batch][1:], 2 * pair + t, x_mx[batch][1:], far)
-            unmasked = results.tile([P, 2, HALF], F32, name="unmasked")
             nc.scalar.activation(
-                out=unmasked[:],
+                out=finished[:, :, far],
                 in_=without_diagonal[:],
                 func=mybir.ActivationFunctionType.Identity,
                 bias=bias[:, 0:1],
             )
-            nc.sync.dma_start(out=rows[:, :, far], in_=unmasked[:])
+            nc.sync.dma_start(
+                out=out[batch, near, :].rearrange("(p t) j -> p (t j)", t=2),
+                in_=finished[:].rearrange("p t j -> p (t j)"),
+            )
 
         for step in range(BATCHES + 2):
             if step < BATCHES:

@@ -33,6 +33,16 @@ def tile_readingorderhead_kernel(tc, panel_embeddings, W_words, W_scales, b, out
         banks = ctx.enter_context(tc.psum_pool(name="banks", bufs=PSUM_BANKS))
         ctx.enter_context(tc.manual_schedule())
 
+        zeros = const.tile([P, PANELS], BF16)
+        nc.vector.memset(zeros[:].bitcast(I32), 0)
+
+        def multiply_zeros(times):
+            unread = banks.tile([P, PANELS], F32, name="bank")
+            for turn in range(times):
+                nc.tensor.matmul(unread[:], lhsT=zeros[:, :P], rhs=zeros[:], start=True, stop=True)
+
+        multiply_zeros(4)
+
         x_rows = []
 
         def load_x(batch, pair):
@@ -194,6 +204,8 @@ def tile_readingorderhead_kernel(tc, panel_embeddings, W_words, W_scales, b, out
         for step in range(BATCHES + 2):
             if step < BATCHES:
                 turn_x(step)
+                if step == 0:
+                    multiply_zeros(2)
                 for pair in range(PAIRS):
                     quantise(x_mx[step], pair)
             for pair in range(PAIRS):

@@ -41,7 +41,7 @@ def tile_readingorderhead_kernel(tc, panel_embeddings, W_words, W_scales, b, out
             for turn in range(times):
                 nc.tensor.matmul(unread[:], lhsT=zeros[:, :P], rhs=zeros[:], start=True, stop=True)
 
-        multiply_zeros(4)
+        multiply_zeros(3)
 
         x_rows = []
 

@@ -93,15 +93,17 @@ def tile_readingorderhead_kernel(tc, panel_embeddings, W_words, W_scales, b, out
         nc.gpsimd.tensor_copy(out=bias[:], in_=bias_bf16[:])
 
         w_scales = const.tile([P, FEATURES], U8, align_bytes=64)
-        nc.vector.tensor_copy(
-            out=w_scales[:].rearrange("p (t m) -> p t m", t=PACK),
-            in_=w_scales_as_sent[:].rearrange("p (m t) -> p t m", t=PACK),
-        )
         w_codes = const.tile([P, FEATURES], U32, align_bytes=64)
-        nc.vector.tensor_copy(
-            out=w_codes[:].bitcast(I32).rearrange("p (t m) -> p t m", t=PACK),
-            in_=w_codes_as_sent[:].bitcast(I32).rearrange("p (m t) -> p t m", t=PACK),
-        )
+
+        def sort_w():
+            nc.vector.tensor_copy(
+                out=w_scales[:].rearrange("p (t m) -> p t m", t=PACK),
+                in_=w_scales_as_sent[:].rearrange("p (m t) -> p t m", t=PACK),
+            )
+            nc.vector.tensor_copy(
+                out=w_codes[:].bitcast(I32).rearrange("p (t m) -> p t m", t=PACK),
+                in_=w_codes_as_sent[:].bitcast(I32).rearrange("p (m t) -> p t m", t=PACK),
+            )
 
         def mx_pass(product, stationary, tile_index, moving, moving_columns):
             columns = slice(tile_index * P, (tile_index + 1) * P)
@@ -133,25 +135,42 @@ def tile_readingorderhead_kernel(tc, panel_embeddings, W_words, W_scales, b, out
         x_mx = {}
         xw_mx = {}
 
-        def turn_x(batch):
-            x_mx[batch] = new_operand("x")
+        sorted_words = {}
+
+        def sort_words(batch, pair):
+            by_parity = const.tile([P, 2, PARITIES, P], I32, name="by_parity")
+            nc.vector.tensor_copy(
+                out=by_parity[:],
+                in_=x_rows[batch][:, 2 * pair : 2 * pair + 2]
+                .bitcast(I32)
+                .rearrange("p t (w u) -> p t u w", u=PARITIES),
+            )
+            sorted_words[batch, pair] = by_parity
+
+        def turn_x(batch, pair):
+            if pair == 0:
+                x_mx[batch] = new_operand("x")
             grouped_words = x_mx[batch][0][:].bitcast(F32).rearrange(
                 "p (h i w) -> p h i w", h=PAIRS, w=2 * PARITIES
             )
-            words = x_rows[batch][:].bitcast(F32)
-            for pair in range(PAIRS):
-                turned = banks.tile([P, 2, PARITIES, P], F32, name="bank")
-                for a in range(2):
-                    for u in range(PARITIES):
-                        nc.tensor.transpose(
-                            turned[:, a, u, :],
-                            words[:, 2 * pair + a, u : FEATURES // 2 : PARITIES],
-                            identity[:],
-                        )
-                nc.scalar.copy(
-                    out=grouped_words[:, pair],
-                    in_=turned[:].rearrange("p t u i -> p i (t u)"),
-                )
+            words = x_rows[batch][:].bitcast(F32).rearrange("p t (w u) -> p t u w", u=PARITIES)
+            first = 2 * pair
+            if (batch, pair) in sorted_words:
+                words = sorted_words[batch, pair][:].bitcast(F32)
+                first = 0
+            turned = banks.tile([P, 2, PARITIES, P], F32, name="bank")
+            for a in range(2):
+                for u in range(PARITIES):
+                    nc.tensor.transpose(
+                        turned[:, a, u, :],
+                        words[:, first + a, u, :],
+                        identity[:],
+                    )
+            copy = nc.scalar.copy
+            copy(
+                out=grouped_words[:, pair],
+                in_=turned[:].rearrange("p t u i -> p i (t u)"),
+            )
 
         def w_times_x(batch, pair):
             if pair == 0:
@@ -201,17 +220,29 @@ def tile_readingorderhead_kernel(tc, panel_embeddings, W_words, W_scales, b, out
                 in_=finished[:].rearrange("p t j -> p (t j)"),
             )
 
+        held = []
+
+        def release():
+            for operand, of_pair in held:
+                quantise(operand, of_pair)
+            held.clear()
+
         for step in range(BATCHES + 2):
-            if step < BATCHES:
-                turn_x(step)
-                if step == 0:
-                    multiply_zeros(2)
-                for pair in range(PAIRS):
+            for pair in range(PAIRS):
+                if step < BATCHES:
+                    turn_x(step, pair)
+                    release()
+                    if step == 0 and pair == 0:
+                        sort_words(1, 0)
+                        sort_w()
                     quantise(x_mx[step], pair)
+            if step == 0:
+                multiply_zeros(2)
             for pair in range(PAIRS):
                 if 0 <= step - 1 < BATCHES:
                     w_times_x(step - 1, pair)
+                    release()
+                    held.append((xw_mx[step - 1], pair))
                 if 0 <= step - 2 < BATCHES:
                     scores(step - 2, pair)
-                if 0 <= step - 1 < BATCHES:
-                    quantise(xw_mx[step - 1], pair)
+                    release()

@@ -184,7 +184,7 @@ def tile_readingorderhead_kernel(tc, panel_embeddings, W_words, W_scales, b, out
                     mx_pass(
                         product[:, t, :], (w_codes, w_scales), t, x_mx[batch][1:], slice(a * P, (a + 1) * P)
                     )
-                to_vector = a == ROW_TILES - 1 if batch == BATCHES - 1 else a % 2 == 1
+                to_vector = a % 2 == 1 if batch % 2 == 0 else a == 1
                 copy = nc.vector.tensor_copy if to_vector else nc.scalar.copy
                 copy(
                     out=places[:, pair, :, a % 2],
@@ -215,34 +215,43 @@ def tile_readingorderhead_kernel(tc, panel_embeddings, W_words, W_scales, b, out
                 func=mybir.ActivationFunctionType.Identity,
                 bias=bias[:, 0:1],
             )
-            nc.sync.dma_start(
-                out=out[batch, near, :].rearrange("(p t) j -> p (t j)", t=2),
-                in_=finished[:].rearrange("p t j -> p (t j)"),
-            )
+            rows = out[batch, near, :].rearrange("(p t) j -> p t j", t=2)
+            for columns in (far, near):
+                nc.sync.dma_start(out=rows[:, :, columns], in_=finished[:, :, columns])
 
         held = []
 
-        def release():
+        def unit(work, batch, pair):
+            work(batch, pair)
             for operand, of_pair in held:
                 quantise(operand, of_pair)
             held.clear()
+            if work is turn_x:
+                held.append((x_mx[batch], pair))
+            elif work is w_times_x:
+                held.append((xw_mx[batch], pair))
 
-        for step in range(BATCHES + 2):
+        def turn_batch(batch):
             for pair in range(PAIRS):
-                if step < BATCHES:
-                    turn_x(step, pair)
-                    release()
-                    if step == 0 and pair == 0:
-                        sort_words(1, 0)
-                        sort_w()
-                    quantise(x_mx[step], pair)
-            if step == 0:
-                multiply_zeros(2)
-            for pair in range(PAIRS):
-                if 0 <= step - 1 < BATCHES:
-                    w_times_x(step - 1, pair)
-                    release()
-                    held.append((xw_mx[step - 1], pair))
-                if 0 <= step - 2 < BATCHES:
-                    scores(step - 2, pair)
-                    release()
+                unit(turn_x, batch, pair)
+                if batch == 0 and pair == 0:
+                    sort_words(1, 0)
+                    sort_w()
+
+        pairs = [(batch, pair) for batch in range(BATCHES) for pair in range(PAIRS)]
+        turn_batch(0)
+        multiply_zeros(2)
+        turn_batch(1)
+        for n in range(2):
+            unit(w_times_x, *pairs[n])
+        turn_batch(2)
+        unit(w_times_x, *pairs[2])
+        for n in range(2):
+            unit(w_times_x, *pairs[n + 3])
+            unit(scores, *pairs[n])
+        turn_batch(3)
+        unit(scores, *pairs[2])
+        for n in range(3, len(pairs)):
+            if n + 2 < len(pairs):
+                unit(w_times_x, *pairs[n + 2])
+            unit(scores, *pairs[n])

@@ -184,7 +184,7 @@ def tile_readingorderhead_kernel(tc, panel_embeddings, W_words, W_scales, b, out
                     mx_pass(
                         product[:, t, :], (w_codes, w_scales), t, x_mx[batch][1:], slice(a * P, (a + 1) * P)
                     )
-                to_vector = a % 2 == 1 if batch % 2 == 0 else a == 1
+                to_vector = a == ROW_TILES - 1 if batch == BATCHES - 1 else a % 2 == 1
                 copy = nc.vector.tensor_copy if to_vector else nc.scalar.copy
                 copy(
                     out=places[:, pair, :, a % 2],
@@ -215,9 +215,10 @@ def tile_readingorderhead_kernel(tc, panel_embeddings, W_words, W_scales, b, out
                 func=mybir.ActivationFunctionType.Identity,
                 bias=bias[:, 0:1],
             )
-            rows = out[batch, near, :].rearrange("(p t) j -> p t j", t=2)
-            for columns in (far, near):
-                nc.sync.dma_start(out=rows[:, :, columns], in_=finished[:, :, columns])
+            nc.sync.dma_start(
+                out=out[batch, near, :].rearrange("(p t) j -> p (t j)", t=2),
+                in_=finished[:].rearrange("p t j -> p (t j)"),
+            )
 
         held = []
 

from contextlib import ExitStack

import concourse.mybir as mybir
from concourse.masks import make_identity

F32 = mybir.dt.float32
BF16 = mybir.dt.bfloat16
I32 = mybir.dt.int32
U32 = mybir.dt.uint32
U8 = mybir.dt.uint8
FP8X4 = mybir.dt.float8_e4m3fn_x4

P = 128
PACK = 4
BATCHES = 4
PANELS = 512
FEATURES = 512
ROW_TILES = PANELS // P
PARITIES = 2
HALF = PANELS // 2
PAIRS = ROW_TILES // 2
PSUM_BANKS = 8

FLOPS = 2 * BATCHES * PANELS * FEATURES * FEATURES + 2 * BATCHES * PANELS * PANELS * FEATURES


def tile_readingorderhead_kernel(tc, panel_embeddings, W_words, W_scales, b, out):
    nc = tc.nc
    with ExitStack() as ctx:
        const = ctx.enter_context(tc.tile_pool(name="const", bufs=1))
        per_batch = ctx.enter_context(tc.tile_pool(name="per_batch", bufs=BATCHES))
        results = ctx.enter_context(tc.tile_pool(name="results", bufs=BATCHES * PAIRS))
        banks = ctx.enter_context(tc.psum_pool(name="banks", bufs=PSUM_BANKS))
        ctx.enter_context(tc.manual_schedule())

        zeros = const.tile([P, PANELS], BF16)
        nc.vector.memset(zeros[:].bitcast(I32), 0)

        def multiply_zeros(times):
            unread = banks.tile([P, PANELS], F32, name="bank")
            for turn in range(times):
                nc.tensor.matmul(unread[:], lhsT=zeros[:, :P], rhs=zeros[:], start=True, stop=True)

        multiply_zeros(3)

        x_rows = []

        def load_x(batch, pair):
            if pair == 0:
                rows = per_batch.tile([P, ROW_TILES, FEATURES], BF16, name="x_rows")
                x_rows.append(rows)
            panels = panel_embeddings[batch].rearrange("(h p t) k -> p h t k", h=PAIRS, t=2)
            nc.sync.dma_start(out=x_rows[batch][:, 2 * pair : 2 * pair + 2], in_=panels[:, pair])

        load_x(0, 0)
        load_x(0, 1)
        load_x(1, 0)
        w_scales_as_sent = const.tile([P, FEATURES], U8, align_bytes=64)
        nc.vector.memset(w_scales_as_sent[:].bitcast(I32), 0)
        for quadrant in range(4):
            nc.sync.dma_start(
                out=w_scales_as_sent[32 * quadrant : 32 * quadrant + 4, :].bitcast(I32),
                in_=W_scales[0, 4 * quadrant : 4 * quadrant + 4, :].bitcast(I32),
            )
        w_codes_as_sent = const.tile([P, FEATURES], U32, align_bytes=64)
        nc.sync.dma_start(
            out=w_codes_as_sent[:].bitcast(I32),
            in_=W_words[0].rearrange("p n t -> p (n t)").bitcast(I32),
        )
        load_x(1, 1)
        load_x(2, 0)
        load_x(2, 1)
        load_x(3, 0)
        load_x(3, 1)

        bias_bf16 = const.tile([P, 1], BF16)
        nc.sync.dma_start(out=bias_bf16[:], in_=b.partition_broadcast(P))
        bias = const.tile([P, 1], F32)

        identity = const.tile([P, P], F32)
        make_identity(nc, identity[:])
        off_diagonal = const.tile([P, 2, HALF], F32)
        nc.vector.memset(off_diagonal[:], 1.0)
        for t in range(2):
            nc.vector.tensor_scalar(
                out=off_diagonal[:, t, t:HALF:2],
                in0=identity[:],
                scalar1=-1.0,
                scalar2=1.0,
                op0=mybir.AluOpType.mult,
                op1=mybir.AluOpType.add,
            )
        nc.gpsimd.tensor_copy(out=bias[:], in_=bias_bf16[:])

        w_scales = const.tile([P, FEATURES], U8, align_bytes=64)
        w_codes = const.tile([P, FEATURES], U32, align_bytes=64)

        def sort_w():
            nc.vector.tensor_copy(
                out=w_scales[:].rearrange("p (t m) -> p t m", t=PACK),
                in_=w_scales_as_sent[:].rearrange("p (m t) -> p t m", t=PACK),
            )
            nc.vector.tensor_copy(
                out=w_codes[:].bitcast(I32).rearrange("p (t m) -> p t m", t=PACK),
                in_=w_codes_as_sent[:].bitcast(I32).rearrange("p (m t) -> p t m", t=PACK),
            )

        def mx_pass(product, stationary, tile_index, moving, moving_columns):
            columns = slice(tile_index * P, (tile_index + 1) * P)
            nc.tensor.matmul_mx(
                out=product,
                lhsT=stationary[0][:, columns].bitcast(FP8X4),
                lhsT_scale=stationary[1][:, columns],
                rhs=moving[0][:, moving_columns].bitcast(FP8X4),
                rhs_scale=moving[1][:, moving_columns],
                start=True,
                stop=True,
            )

        def new_operand(kind):
            grouped = per_batch.tile([P, PACK * PANELS], BF16, name=kind + "_grouped", align_bytes=64)
            codes = per_batch.tile([P, PANELS], U32, name=kind + "_codes", align_bytes=64)
            scales = per_batch.tile([P, PANELS], U8, name=kind + "_scales", align_bytes=64)
            return grouped, codes, scales

        def quantise(operand, pair):
            grouped, codes, scales = operand
            panels = slice(pair * HALF, (pair + 1) * HALF)
            nc.vector.quantize_mx(
                out=codes[:, panels].bitcast(FP8X4),
                scales=scales[:, panels],
                in_=grouped[:, PACK * pair * HALF : PACK * (pair + 1) * HALF],
            )

        x_mx = {}
        xw_mx = {}

        sorted_words = {}

        def sort_words(batch, pair):
            by_parity = const.tile([P, 2, PARITIES, P], I32, name="by_parity")
            nc.vector.tensor_copy(
                out=by_parity[:],
                in_=x_rows[batch][:, 2 * pair : 2 * pair + 2]
                .bitcast(I32)
                .rearrange("p t (w u) -> p t u w", u=PARITIES),
            )
            sorted_words[batch, pair] = by_parity

        def turn_x(batch, pair):
            if pair == 0:
                x_mx[batch] = new_operand("x")
            grouped_words = x_mx[batch][0][:].bitcast(F32).rearrange(
                "p (h i w) -> p h i w", h=PAIRS, w=2 * PARITIES
            )
            words = x_rows[batch][:].bitcast(F32).rearrange("p t (w u) -> p t u w", u=PARITIES)
            first = 2 * pair
            if (batch, pair) in sorted_words:
                words = sorted_words[batch, pair][:].bitcast(F32)
                first = 0
            turned = banks.tile([P, 2, PARITIES, P], F32, name="bank")
            for a in range(2):
                for u in range(PARITIES):
                    nc.tensor.transpose(
                        turned[:, a, u, :],
                        words[:, first + a, u, :],
                        identity[:],
                    )
            copy = nc.scalar.copy
            copy(
                out=grouped_words[:, pair],
                in_=turned[:].rearrange("p t u i -> p i (t u)"),
            )

        def w_times_x(batch, pair):
            if pair == 0:
                xw_mx[batch] = new_operand("xw")
            places = xw_mx[batch][0][:].rearrange(
                "p (h e c i t) -> p h e c i t", h=PAIRS, e=2, c=2, t=PACK
            )
            for a in range(2 * pair, 2 * pair + 2):
                product = banks.tile([P, PACK, P], F32, name="bank")
                for t in range(PACK):
                    mx_pass(
                        product[:, t, :], (w_codes, w_scales), t, x_mx[batch][1:], slice(a * P, (a + 1) * P)
                    )
                to_vector = a == ROW_TILES - 1 if batch == BATCHES - 1 else a % 2 == 1
                copy = nc.vector.tensor_copy if to_vector else nc.scalar.copy
                copy(
                    out=places[:, pair, :, a % 2],
                    in_=product[:].rearrange("p t (i e) -> p e i t", e=2),
                )

        def scores(batch, pair):
            near = slice(pair * HALF, (pair + 1) * HALF)
            far = slice((1 - pair) * HALF, (2 - pair) * HALF)
            finished = results.tile([P, 2, PANELS], F32, name="finished")
            with_diagonal = banks.tile([P, 2, HALF], F32, name="bank")
            for t in range(2):
                mx_pass(with_diagonal[:, t, :], xw_mx[batch][1:], 2 * pair + t, x_mx[batch][1:], near)
            nc.vector.scalar_tensor_tensor(
                out=finished[:, :, near],
                in0=with_diagonal[:],
                scalar=bias[:, 0:1],
                in1=off_diagonal[:],
                op0=mybir.AluOpType.add,
                op1=mybir.AluOpType.mult,
            )
            without_diagonal = banks.tile([P, 2, HALF], F32, name="bank")
            for t in range(2):
                mx_pass(without_diagonal[:, t, :], xw_mx[batch][1:], 2 * pair + t, x_mx[batch][1:], far)
            nc.scalar.activation(
                out=finished[:, :, far],
                in_=without_diagonal[:],
                func=mybir.ActivationFunctionType.Identity,
                bias=bias[:, 0:1],
            )
            nc.sync.dma_start(
                out=out[batch, near, :].rearrange("(p t) j -> p (t j)", t=2),
                in_=finished[:].rearrange("p t j -> p (t j)"),
            )

        held = []

        def unit(work, batch, pair):
            work(batch, pair)
            for operand, of_pair in held:
                quantise(operand, of_pair)
            held.clear()
            if work is turn_x:
                held.append((x_mx[batch], pair))
            elif work is w_times_x:
                held.append((xw_mx[batch], pair))

        def turn_batch(batch):
            for pair in range(PAIRS):
                unit(turn_x, batch, pair)
                if batch == 0 and pair == 0:
                    sort_words(1, 0)
                    sort_w()

        pairs = [(batch, pair) for batch in range(BATCHES) for pair in range(PAIRS)]
        turn_batch(0)
        multiply_zeros(2)
        turn_batch(1)
        for n in range(2):
            unit(w_times_x, *pairs[n])
        turn_batch(2)
        unit(w_times_x, *pairs[2])
        for n in range(2):
            unit(w_times_x, *pairs[n + 3])
            unit(scores, *pairs[n])
        turn_batch(3)
        unit(scores, *pairs[2])
        for n in range(3, len(pairs)):
            if n + 2 < len(pairs):
                unit(w_times_x, *pairs[n + 2])
            unit(scores, *pairs[n])
